import numpy as np
import ml_dtypes


def mxq(x, axis, fmt="e4m3"):
    dtype, down = {"e4m3": (ml_dtypes.float8_e4m3fn, 7), "e5m2": (ml_dtypes.float8_e5m2, 14)}[fmt]
    v = np.moveaxis(np.asarray(x, np.float32).astype(ml_dtypes.bfloat16).astype(np.float64), axis, -1)
    blocks = v.reshape(v.shape[:-1] + (-1, 32))
    amax = np.abs(blocks).max(-1, keepdims=True)
    byte = np.maximum(np.where(amax > 0, np.frexp(amax)[1] - 1 + 127, 0) - down, 1)
    scale = np.exp2(byte - 127.0)
    codes = (blocks / scale).astype(np.float32).astype(dtype).astype(np.float64)
    return np.moveaxis((codes * scale).reshape(v.shape), -1, axis)


WIDE = False


def mx_kscale(k):
    if not WIDE:
        return np.ones(k)
    levels = np.array([20, -20, 10, -10, 0])
    a = np.random.permutation(np.resize(levels, k // 512 * 4)).reshape(k // 512, 4)
    idx = np.arange(k)
    return np.exp2(a[idx // 512, idx % 128 // 32])


BF16 = ml_dtypes.bfloat16


def bf(x):
    return np.asarray(x, np.float32).astype(BF16)


def f64(x):
    return np.asarray(x).astype(np.float64)


B, S, IN_F, OUT_F, GROUP_SIZE = 4, 2048, 1024, 512, 128
T = B * S


def setup_inputs():
    s = mx_kscale(T).reshape(B, S, 1)
    x = np.random.standard_normal((B, S, IN_F)) * s
    sw = np.sign(np.random.standard_normal((OUT_F, IN_F)))
    sw = np.where(sw == 0, 1.0, sw)
    scales = np.random.uniform(0.32, 3.2, OUT_F * IN_F // GROUP_SIZE) / np.sqrt(IN_F)
    g = np.random.standard_normal((B, S, OUT_F)) * np.exp2(np.random.randint(-12, 1, (B, S, 1))) / s
    return {"x": bf(x), "sign_weights": bf(sw), "scales": bf(scales), "grad_out": bf(g)}


def reference(x, sign_weights, scales, grad_out):
    xt = f64(x).reshape(T, IN_F)
    gt = f64(grad_out).reshape(T, OUT_F)
    scale_mat = np.repeat(f64(scales), GROUP_SIZE).reshape(OUT_F, IN_F)
    gw = mxq(gt, 0, "e5m2").T @ mxq(xt, 0, "e4m3")
    return gw * scale_mat

@@ -1,0 +1,182 @@
+from contextlib import ExitStack
+
+import concourse.mybir as mybir
+
+BF16 = mybir.dt.bfloat16
+F32 = mybir.dt.float32
+U32 = mybir.dt.uint32
+U8 = mybir.dt.uint8
+E4M3X4 = mybir.dt.float8_e4m3fn_x4
+E5M2X4 = mybir.dt.float8_e5m2_x4
+
+P = 128
+PACK = 4
+K_PASS = P * PACK
+TOKENS = 8192
+IN_F = 1024
+OUT_F = 512
+GROUP = 128
+N_TILE = 512
+M_TILE = 128
+CHUNKS = TOKENS // K_PASS
+O_TILES = OUT_F // M_TILE
+I_TILES = IN_F // N_TILE
+GROUPS_PER_ROW = IN_F // GROUP
+GROUPS_PER_BANK = N_TILE // GROUP
+RUN = 4
+
+RAW_BUFS = 6
+X_SCALAR = 768
+VECTOR_BANKS = (3, 4, 5, 7)
+
+FLOPS = 2 * TOKENS * IN_F * OUT_F
+BYTES = 2 * TOKENS * (IN_F + OUT_F) + 2 * OUT_F * GROUPS_PER_ROW + 4 * OUT_F * IN_F
+
+
+def regroup(copy, dst, src, lo, hi):
+    copy(
+        out=dst[:, lo:hi, :].rearrange("p (c i) t -> p c t i", i=RUN),
+        in_=src[:, :, lo:hi].rearrange("p t (c i) -> p c t i", i=RUN),
+    )
+
+
+def tile_stebitlinear_t_kernel(tc, x, sign_weights, scales, grad_out, out):
+    nc = tc.nc
+    xt = x.flatten_outer_dims()
+    gt = grad_out.flatten_outer_dims()
+    last = CHUNKS - 1
+
+    with ExitStack() as ctx:
+        const = ctx.enter_context(tc.tile_pool(name="const", bufs=1))
+        raw = ctx.enter_context(tc.tile_pool(name="raw", bufs=RAW_BUFS))
+        grp = ctx.enter_context(tc.tile_pool(name="grp", bufs=3))
+        cod = ctx.enter_context(tc.tile_pool(name="cod", bufs=3))
+        res = ctx.enter_context(tc.tile_pool(name="res", bufs=O_TILES * I_TILES))
+        psum = ctx.enter_context(tc.psum_pool(name="psum", bufs=1))
+        ctx.enter_context(tc.manual_schedule())
+
+        raw_x = {}
+        raw_g = {}
+        grp_x = {}
+        grp_g = {}
+        cod_x = {}
+        cod_g = {}
+
+        sc_bf = const.tile([P, O_TILES * GROUPS_PER_ROW], BF16, name="sc_bf")
+        nc.scalar.dma_start(
+            out=sc_bf[:].rearrange("p (t g) -> p t g", g=GROUPS_PER_ROW),
+            in_=scales.rearrange("(t p g) -> p t g", p=P, g=GROUPS_PER_ROW),
+        )
+        sc32 = const.tile([P, O_TILES * GROUPS_PER_ROW], F32, name="sc32")
+        nc.scalar.activation(out=sc32[:], in_=sc_bf[:], func=mybir.ActivationFunctionType.Copy)
+
+        acc = {}
+        for ih in range(I_TILES):
+            for ot in range(O_TILES):
+                acc[(ot, ih)] = psum.tile([P, N_TILE], F32, name="acc_%d_%d" % (ot, ih))
+
+        def load(c):
+            rows = slice(c * K_PASS, (c + 1) * K_PASS)
+            g_raw = raw.tile([P, PACK, OUT_F], BF16, name="g_raw", tag="g_raw")
+            nc.sync.dma_start(out=g_raw[:], in_=gt[rows, :].rearrange("(p j) w -> p j w", j=PACK))
+            x_raw = raw.tile([P, PACK, IN_F], BF16, name="x_raw", tag="x_raw")
+            nc.sync.dma_start(out=x_raw[:], in_=xt[rows, :].rearrange("(p j) w -> p j w", j=PACK))
+            raw_g[c] = g_raw
+            raw_x[c] = x_raw
+
+        def copies(c):
+            g_grp = grp.tile([P, OUT_F, PACK], BF16, name="g_grp", tag="g_grp", align_bytes=64)
+            x_grp = grp.tile([P, IN_F, PACK], BF16, name="x_grp", tag="x_grp", align_bytes=64)
+            grp_g[c] = g_grp
+            grp_x[c] = x_grp
+            regroup(nc.vector.tensor_copy, g_grp, raw_g[c], 0, OUT_F)
+            regroup(nc.vector.tensor_copy, x_grp, raw_x[c], X_SCALAR, IN_F)
+            if c == last:
+                regroup(nc.scalar.copy, x_grp, raw_x[c], 0, N_TILE)
+                regroup(nc.scalar.copy, x_grp, raw_x[c], N_TILE, X_SCALAR)
+            else:
+                regroup(nc.scalar.copy, x_grp, raw_x[c], 0, X_SCALAR)
+
+        def quantise_g(c):
+            g_cod = cod.tile([P, OUT_F], U32, name="g_cod", tag="g_cod", align_bytes=64)
+            g_scl = cod.tile([P, OUT_F], U8, name="g_scl", tag="g_scl", align_bytes=64)
+            cod_g[c] = (g_cod, g_scl)
+            nc.vector.quantize_mx(
+                out=g_cod[:].bitcast(E5M2X4),
+                scales=g_scl[:],
+                in_=grp_g[c][:].rearrange("p w j -> p (w j)"),
+            )
+
+        def quantise_x(c):
+            x_cod = cod.tile([P, IN_F], U32, name="x_cod", tag="x_cod", align_bytes=64)
+            x_scl = cod.tile([P, IN_F], U8, name="x_scl", tag="x_scl", align_bytes=64)
+            cod_x[c] = (x_cod, x_scl)
+            pieces = I_TILES if c == last else 1
+            width = IN_F // pieces
+            for h in range(pieces):
+                cols = slice(h * width, (h + 1) * width)
+                nc.vector.quantize_mx(
+                    out=x_cod[:, cols].bitcast(E4M3X4),
+                    scales=x_scl[:, cols],
+                    in_=grp_x[c][:, cols, :].rearrange("p w j -> p (w j)"),
+                )
+
+        def passes(c):
+            g_cod, g_scl = cod_g[c]
+            x_cod, x_scl = cod_x[c]
+            for ih in range(I_TILES):
+                n_cols = slice(ih * N_TILE, (ih + 1) * N_TILE)
+                for ot in range(O_TILES):
+                    m_cols = slice(ot * M_TILE, (ot + 1) * M_TILE)
+                    nc.tensor.matmul_mx(
+                        out=acc[(ot, ih)][:],
+                        lhsT=g_cod[:, m_cols].bitcast(E5M2X4),
+                        lhsT_scale=g_scl[:, m_cols],
+                        rhs=x_cod[:, n_cols].bitcast(E4M3X4),
+                        rhs_scale=x_scl[:, n_cols],
+                        start=(c == 0),
+                        stop=(c == last),
+                    )
+
+        for c in range(RAW_BUFS - 1):
+            load(c)
+        for c in range(CHUNKS + 1):
+            if c + RAW_BUFS - 1 < CHUNKS:
+                load(c + RAW_BUFS - 1)
+            if c < CHUNKS:
+                copies(c)
+            if c >= 1:
+                quantise_x(c - 1)
+            if c < CHUNKS:
+                quantise_g(c)
+            if c >= 1:
+                passes(c - 1)
+
+        bank = 0
+        for ih in range(I_TILES):
+            for ot in range(O_TILES):
+                first = ot * GROUPS_PER_ROW + ih * GROUPS_PER_BANK
+                scaled = res.tile([P, N_TILE], F32, name="scaled", tag="scaled")
+                if bank in VECTOR_BANKS:
+                    nc.vector.tensor_tensor(
+                        out=scaled[:].rearrange("p (g w) -> p g w", g=GROUPS_PER_BANK),
+                        in0=acc[(ot, ih)][:].rearrange("p (g w) -> p g w", g=GROUPS_PER_BANK),
+                        in1=sc32[:, first : first + GROUPS_PER_BANK]
+                        .unsqueeze(2)
+                        .to_broadcast([P, GROUPS_PER_BANK, GROUP]),
+                        op=mybir.AluOpType.mult,
+                    )
+                else:
+                    for g in range(GROUPS_PER_BANK):
+                        cols = slice(g * GROUP, (g + 1) * GROUP)
+                        nc.scalar.activation(
+                            out=scaled[:, cols],
+                            in_=acc[(ot, ih)][:, cols],
+                            func=mybir.ActivationFunctionType.Copy,
+                            scale=sc32[:, first + g : first + g + 1],
+                        )
+                nc.sync.dma_start(
+                    out=out[ot * M_TILE : (ot + 1) * M_TILE, ih * N_TILE : (ih + 1) * N_TILE],
+                    in_=scaled[:],
+                )
+                bank += 1

@@ -26,8 +26,10 @@ GROUPS_PER_BANK = N_TILE // GROUP
 RUN = 4
 
 RAW_BUFS = 6
-X_SCALAR = 768
-VECTOR_BANKS = (3, 4, 5, 7)
+X_SCALAR = 792
+HEAD_VECTOR = 248
+TAIL_SCALAR = 384
+OUT_ORDER = ((0, "s"), (2, "v"), (1, "s"), (3, "v"), (4, "s"), (6, "v"), (5, "s"), (7, "v"))
 
 FLOPS = 2 * TOKENS * IN_F * OUT_F
 BYTES = 2 * TOKENS * (IN_F + OUT_F) + 2 * OUT_F * GROUPS_PER_ROW + 4 * OUT_F * IN_F
@@ -75,56 +77,65 @@ def tile_stebitlinear_t_kernel(tc, x, sign_weights, scales, grad_out, out):
             for ot in range(O_TILES):
                 acc[(ot, ih)] = psum.tile([P, N_TILE], F32, name="acc_%d_%d" % (ot, ih))
 
-        def load(c):
+        def load(c, x_pieces):
             rows = slice(c * K_PASS, (c + 1) * K_PASS)
             g_raw = raw.tile([P, PACK, OUT_F], BF16, name="g_raw", tag="g_raw")
             nc.sync.dma_start(out=g_raw[:], in_=gt[rows, :].rearrange("(p j) w -> p j w", j=PACK))
             x_raw = raw.tile([P, PACK, IN_F], BF16, name="x_raw", tag="x_raw")
-            nc.sync.dma_start(out=x_raw[:], in_=xt[rows, :].rearrange("(p j) w -> p j w", j=PACK))
+            width = IN_F // x_pieces
+            for h in range(x_pieces):
+                cols = slice(h * width, (h + 1) * width)
+                nc.sync.dma_start(
+                    out=x_raw[:, :, cols],
+                    in_=xt[rows, cols].rearrange("(p j) w -> p j w", j=PACK),
+                )
             raw_g[c] = g_raw
             raw_x[c] = x_raw
 
-        def copies(c):
-            g_grp = grp.tile([P, OUT_F, PACK], BF16, name="g_grp", tag="g_grp", align_bytes=64)
-            x_grp = grp.tile([P, IN_F, PACK], BF16, name="x_grp", tag="x_grp", align_bytes=64)
-            grp_g[c] = g_grp
-            grp_x[c] = x_grp
-            regroup(nc.vector.tensor_copy, g_grp, raw_g[c], 0, OUT_F)
-            regroup(nc.vector.tensor_copy, x_grp, raw_x[c], X_SCALAR, IN_F)
-            if c == last:
-                regroup(nc.scalar.copy, x_grp, raw_x[c], 0, N_TILE)
-                regroup(nc.scalar.copy, x_grp, raw_x[c], N_TILE, X_SCALAR)
-            else:
-                regroup(nc.scalar.copy, x_grp, raw_x[c], 0, X_SCALAR)
+        def open_chunk(c):
+            grp_g[c] = grp.tile([P, OUT_F, PACK], BF16, name="g_grp", tag="g_grp", align_bytes=64)
+            grp_x[c] = grp.tile([P, IN_F, PACK], BF16, name="x_grp", tag="x_grp", align_bytes=64)
+            cod_g[c] = (
+                cod.tile([P, OUT_F], U32, name="g_cod", tag="g_cod", align_bytes=64),
+                cod.tile([P, OUT_F], U8, name="g_scl", tag="g_scl", align_bytes=64),
+            )
+            cod_x[c] = (
+                cod.tile([P, IN_F], U32, name="x_cod", tag="x_cod", align_bytes=64),
+                cod.tile([P, IN_F], U8, name="x_scl", tag="x_scl", align_bytes=64),
+            )
+
+        def vector_g(c, lo, hi):
+            regroup(nc.vector.tensor_copy, grp_g[c], raw_g[c], lo, hi)
+
+        def scalar_g(c, lo, hi):
+            regroup(nc.scalar.copy, grp_g[c], raw_g[c], lo, hi)
+
+        def vector_x(c, lo, hi):
+            regroup(nc.vector.tensor_copy, grp_x[c], raw_x[c], lo, hi)
+
+        def scalar_x(c, lo, hi):
+            regroup(nc.scalar.copy, grp_x[c], raw_x[c], lo, hi)
 
         def quantise_g(c):
-            g_cod = cod.tile([P, OUT_F], U32, name="g_cod", tag="g_cod", align_bytes=64)
-            g_scl = cod.tile([P, OUT_F], U8, name="g_scl", tag="g_scl", align_bytes=64)
-            cod_g[c] = (g_cod, g_scl)
+            g_cod, g_scl = cod_g[c]
             nc.vector.quantize_mx(
                 out=g_cod[:].bitcast(E5M2X4),
                 scales=g_scl[:],
                 in_=grp_g[c][:].rearrange("p w j -> p (w j)"),
             )
 
-        def quantise_x(c):
-            x_cod = cod.tile([P, IN_F], U32, name="x_cod", tag="x_cod", align_bytes=64)
-            x_scl = cod.tile([P, IN_F], U8, name="x_scl", tag="x_scl", align_bytes=64)
-            cod_x[c] = (x_cod, x_scl)
-            pieces = I_TILES if c == last else 1
-            width = IN_F // pieces
-            for h in range(pieces):
-                cols = slice(h * width, (h + 1) * width)
-                nc.vector.quantize_mx(
-                    out=x_cod[:, cols].bitcast(E4M3X4),
-                    scales=x_scl[:, cols],
-                    in_=grp_x[c][:, cols, :].rearrange("p w j -> p (w j)"),
-                )
+        def quantise_x(c, lo, hi):
+            x_cod, x_scl = cod_x[c]
+            nc.vector.quantize_mx(
+                out=x_cod[:, lo:hi].bitcast(E4M3X4),
+                scales=x_scl[:, lo:hi],
+                in_=grp_x[c][:, lo:hi, :].rearrange("p w j -> p (w j)"),
+            )
 
-        def passes(c):
+        def passes(c, halves):
             g_cod, g_scl = cod_g[c]
             x_cod, x_scl = cod_x[c]
-            for ih in range(I_TILES):
+            for ih in halves:
                 n_cols = slice(ih * N_TILE, (ih + 1) * N_TILE)
                 for ot in range(O_TILES):
                     m_cols = slice(ot * M_TILE, (ot + 1) * M_TILE)
@@ -138,45 +149,72 @@ def tile_stebitlinear_t_kernel(tc, x, sign_weights, scales, grad_out, out):
                         stop=(c == last),
                     )
 
-        for c in range(RAW_BUFS - 1):
-            load(c)
-        for c in range(CHUNKS + 1):
-            if c + RAW_BUFS - 1 < CHUNKS:
-                load(c + RAW_BUFS - 1)
-            if c < CHUNKS:
-                copies(c)
-            if c >= 1:
-                quantise_x(c - 1)
-            if c < CHUNKS:
-                quantise_g(c)
-            if c >= 1:
-                passes(c - 1)
+        load(0, I_TILES)
+        for c in range(1, RAW_BUFS):
+            load(c, 1)
+        open_chunk(0)
+        vector_g(0, 0, HEAD_VECTOR)
+        scalar_g(0, HEAD_VECTOR, OUT_F)
+        vector_x(0, 0, HEAD_VECTOR)
+        scalar_x(0, HEAD_VECTOR, N_TILE)
+        quantise_g(0)
+        vector_x(0, N_TILE, N_TILE + HEAD_VECTOR)
+        scalar_x(0, N_TILE + HEAD_VECTOR, IN_F)
+        quantise_x(0, 0, N_TILE)
+        passes(0, (0,))
 
-        bank = 0
-        for ih in range(I_TILES):
-            for ot in range(O_TILES):
-                first = ot * GROUPS_PER_ROW + ih * GROUPS_PER_BANK
-                scaled = res.tile([P, N_TILE], F32, name="scaled", tag="scaled")
-                if bank in VECTOR_BANKS:
-                    nc.vector.tensor_tensor(
-                        out=scaled[:].rearrange("p (g w) -> p g w", g=GROUPS_PER_BANK),
-                        in0=acc[(ot, ih)][:].rearrange("p (g w) -> p g w", g=GROUPS_PER_BANK),
-                        in1=sc32[:, first : first + GROUPS_PER_BANK]
-                        .unsqueeze(2)
-                        .to_broadcast([P, GROUPS_PER_BANK, GROUP]),
-                        op=mybir.AluOpType.mult,
-                    )
-                else:
-                    for g in range(GROUPS_PER_BANK):
-                        cols = slice(g * GROUP, (g + 1) * GROUP)
-                        nc.scalar.activation(
-                            out=scaled[:, cols],
-                            in_=acc[(ot, ih)][:, cols],
-                            func=mybir.ActivationFunctionType.Copy,
-                            scale=sc32[:, first + g : first + g + 1],
-                        )
-                nc.sync.dma_start(
-                    out=out[ot * M_TILE : (ot + 1) * M_TILE, ih * N_TILE : (ih + 1) * N_TILE],
-                    in_=scaled[:],
+        for c in range(1, last):
+            if c + RAW_BUFS - 1 < CHUNKS:
+                load(c + RAW_BUFS - 1, 1)
+            open_chunk(c)
+            vector_g(c, 0, OUT_F)
+            scalar_x(c, 0, X_SCALAR)
+            if c == 1:
+                quantise_x(0, N_TILE, IN_F)
+                passes(0, (1,))
+            else:
+                quantise_x(c - 1, 0, IN_F)
+                passes(c - 1, (0, 1))
+            vector_x(c, X_SCALAR, IN_F)
+            quantise_g(c)
+
+        open_chunk(last)
+        quantise_x(last - 1, 0, IN_F)
+        passes(last - 1, (0, 1))
+        vector_g(last, 0, OUT_F)
+        scalar_x(last, 0, N_TILE)
+        quantise_x(last, 0, N_TILE)
+        quantise_g(last)
+        passes(last, (0,))
+        scalar_x(last, N_TILE, N_TILE + TAIL_SCALAR)
+        vector_x(last, N_TILE + TAIL_SCALAR, IN_F)
+        quantise_x(last, N_TILE, IN_F)
+        passes(last, (1,))
+
+        for bank, engine in OUT_ORDER:
+            ih = bank // O_TILES
+            ot = bank % O_TILES
+            first = ot * GROUPS_PER_ROW + ih * GROUPS_PER_BANK
+            scaled = res.tile([P, N_TILE], F32, name="scaled", tag="scaled")
+            if engine == "v":
+                nc.vector.tensor_tensor(
+                    out=scaled[:].rearrange("p (g w) -> p g w", g=GROUPS_PER_BANK),
+                    in0=acc[(ot, ih)][:].rearrange("p (g w) -> p g w", g=GROUPS_PER_BANK),
+                    in1=sc32[:, first : first + GROUPS_PER_BANK]
+                    .unsqueeze(2)
+                    .to_broadcast([P, GROUPS_PER_BANK, GROUP]),
+                    op=mybir.AluOpType.mult,
                 )
-                bank += 1
+            else:
+                for g in range(GROUPS_PER_BANK):
+                    cols = slice(g * GROUP, (g + 1) * GROUP)
+                    nc.scalar.activation(
+                        out=scaled[:, cols],
+                        in_=acc[(ot, ih)][:, cols],
+                        func=mybir.ActivationFunctionType.Copy,
+                        scale=sc32[:, first + g : first + g + 1],
+                    )
+            nc.sync.dma_start(
+                out=out[ot * M_TILE : (ot + 1) * M_TILE, ih * N_TILE : (ih + 1) * N_TILE],
+                in_=scaled[:],
+            )

@@ -26,7 +26,7 @@ GROUPS_PER_BANK = N_TILE // GROUP
 RUN = 4
 
 RAW_BUFS = 6
-X_SCALAR = 792
+X_SCALAR = 736
 HEAD_VECTOR = 248
 TAIL_SCALAR = 384
 OUT_ORDER = ((0, "s"), (2, "v"), (1, "s"), (3, "v"), (4, "s"), (6, "v"), (5, "s"), (7, "v"))

@@ -26,6 +26,8 @@ GROUPS_PER_BANK = N_TILE // GROUP
 RUN = 4
 
 RAW_BUFS = 6
+SCALES_LOADED = 8
+SCALES_WIDENED = 11
 X_SCALAR = 736
 HEAD_VECTOR = 248
 TAIL_SCALAR = 384
@@ -65,32 +67,48 @@ def tile_stebitlinear_t_kernel(tc, x, sign_weights, scales, grad_out, out):
         cod_g = {}
 
         sc_bf = const.tile([P, O_TILES * GROUPS_PER_ROW], BF16, name="sc_bf")
-        nc.scalar.dma_start(
-            out=sc_bf[:].rearrange("p (t g) -> p t g", g=GROUPS_PER_ROW),
-            in_=scales.rearrange("(t p g) -> p t g", p=P, g=GROUPS_PER_ROW),
-        )
         sc32 = const.tile([P, O_TILES * GROUPS_PER_ROW], F32, name="sc32")
-        nc.scalar.activation(out=sc32[:], in_=sc_bf[:], func=mybir.ActivationFunctionType.Copy)
+
+        def load_scales():
+            nc.scalar.dma_start(
+                out=sc_bf[:].rearrange("p (t g) -> p t g", g=GROUPS_PER_ROW),
+                in_=scales.rearrange("(t p g) -> p t g", p=P, g=GROUPS_PER_ROW),
+            )
+
+        def widen_scales():
+            nc.scalar.activation(out=sc32[:], in_=sc_bf[:], func=mybir.ActivationFunctionType.Copy)
 
         acc = {}
         for ih in range(I_TILES):
             for ot in range(O_TILES):
                 acc[(ot, ih)] = psum.tile([P, N_TILE], F32, name="acc_%d_%d" % (ot, ih))
 
-        def load(c, x_pieces):
+        def load_g(c):
             rows = slice(c * K_PASS, (c + 1) * K_PASS)
-            g_raw = raw.tile([P, PACK, OUT_F], BF16, name="g_raw", tag="g_raw")
-            nc.sync.dma_start(out=g_raw[:], in_=gt[rows, :].rearrange("(p j) w -> p j w", j=PACK))
-            x_raw = raw.tile([P, PACK, IN_F], BF16, name="x_raw", tag="x_raw")
-            width = IN_F // x_pieces
-            for h in range(x_pieces):
-                cols = slice(h * width, (h + 1) * width)
-                nc.sync.dma_start(
-                    out=x_raw[:, :, cols],
-                    in_=xt[rows, cols].rearrange("(p j) w -> p j w", j=PACK),
-                )
-            raw_g[c] = g_raw
-            raw_x[c] = x_raw
+            raw_g[c] = raw.tile([P, PACK, OUT_F], BF16, name="g_raw", tag="g_raw")
+            nc.sync.dma_start(out=raw_g[c][:], in_=gt[rows, :].rearrange("(p j) w -> p j w", j=PACK))
+
+        def load_x(c):
+            rows = slice(c * K_PASS, (c + 1) * K_PASS)
+            raw_x[c] = raw.tile([P, PACK, IN_F], BF16, name="x_raw", tag="x_raw")
+            nc.sync.dma_start(out=raw_x[c][:], in_=xt[rows, :].rearrange("(p j) w -> p j w", j=PACK))
+
+        first_x = [
+            const.tile([P, PACK, N_TILE], BF16, name="first_x_%d" % ih) for ih in range(I_TILES)
+        ]
+
+        def load_first_x(ih):
+            cols = slice(ih * N_TILE, (ih + 1) * N_TILE)
+            nc.sync.dma_start(
+                out=first_x[ih][:], in_=xt[0:K_PASS, cols].rearrange("(p j) w -> p j w", j=PACK)
+            )
+
+        def first_x_regroup(copy, ih, lo, hi):
+            cols = slice(ih * N_TILE + lo, ih * N_TILE + hi)
+            copy(
+                out=grp_x[0][:, cols, :].rearrange("p (c i) t -> p c t i", i=RUN),
+                in_=first_x[ih][:, :, lo:hi].rearrange("p t (c i) -> p c t i", i=RUN),
+            )
 
         def open_chunk(c):
             grp_g[c] = grp.tile([P, OUT_F, PACK], BF16, name="g_grp", tag="g_grp", align_bytes=64)
@@ -149,23 +167,31 @@ def tile_stebitlinear_t_kernel(tc, x, sign_weights, scales, grad_out, out):
                         stop=(c == last),
                     )
 
-        load(0, I_TILES)
+        load_g(0)
+        for ih in range(I_TILES):
+            load_first_x(ih)
         for c in range(1, RAW_BUFS):
-            load(c, 1)
+            load_g(c)
+            load_x(c)
         open_chunk(0)
         vector_g(0, 0, HEAD_VECTOR)
         scalar_g(0, HEAD_VECTOR, OUT_F)
-        vector_x(0, 0, HEAD_VECTOR)
-        scalar_x(0, HEAD_VECTOR, N_TILE)
+        first_x_regroup(nc.vector.tensor_copy, 0, 0, HEAD_VECTOR)
+        first_x_regroup(nc.scalar.copy, 0, HEAD_VECTOR, N_TILE)
         quantise_g(0)
-        vector_x(0, N_TILE, N_TILE + HEAD_VECTOR)
-        scalar_x(0, N_TILE + HEAD_VECTOR, IN_F)
+        first_x_regroup(nc.vector.tensor_copy, 1, 0, HEAD_VECTOR)
+        first_x_regroup(nc.scalar.copy, 1, HEAD_VECTOR, N_TILE)
         quantise_x(0, 0, N_TILE)
         passes(0, (0,))
 
         for c in range(1, last):
             if c + RAW_BUFS - 1 < CHUNKS:
-                load(c + RAW_BUFS - 1, 1)
+                load_g(c + RAW_BUFS - 1)
+                load_x(c + RAW_BUFS - 1)
+            if c == SCALES_LOADED:
+                load_scales()
+            if c == SCALES_WIDENED:
+                widen_scales()
             open_chunk(c)
             vector_g(c, 0, OUT_F)
             scalar_x(c, 0, X_SCALAR)

@@ -30,8 +30,7 @@ SCALES_LOADED = 8
 SCALES_WIDENED = 11
 X_SCALAR = 736
 HEAD_VECTOR = 248
-TAIL_SCALAR = 384
-OUT_ORDER = ((0, "s"), (2, "v"), (1, "s"), (3, "v"), (4, "s"), (6, "v"), (5, "s"), (7, "v"))
+TAIL_X_SCALAR = 512
 
 FLOPS = 2 * TOKENS * IN_F * OUT_F
 BYTES = 2 * TOKENS * (IN_F + OUT_F) + 2 * OUT_F * GROUPS_PER_ROW + 4 * OUT_F * IN_F
@@ -134,12 +133,12 @@ def tile_stebitlinear_t_kernel(tc, x, sign_weights, scales, grad_out, out):
         def scalar_x(c, lo, hi):
             regroup(nc.scalar.copy, grp_x[c], raw_x[c], lo, hi)
 
-        def quantise_g(c):
+        def quantise_g(c, lo, hi):
             g_cod, g_scl = cod_g[c]
             nc.vector.quantize_mx(
-                out=g_cod[:].bitcast(E5M2X4),
-                scales=g_scl[:],
-                in_=grp_g[c][:].rearrange("p w j -> p (w j)"),
+                out=g_cod[:, lo:hi].bitcast(E5M2X4),
+                scales=g_scl[:, lo:hi],
+                in_=grp_g[c][:, lo:hi, :].rearrange("p w j -> p (w j)"),
             )
 
         def quantise_x(c, lo, hi):
@@ -150,12 +149,12 @@ def tile_stebitlinear_t_kernel(tc, x, sign_weights, scales, grad_out, out):
                 in_=grp_x[c][:, lo:hi, :].rearrange("p w j -> p (w j)"),
             )
 
-        def passes(c, halves):
+        def passes(c, halves, o_tiles=range(O_TILES)):
             g_cod, g_scl = cod_g[c]
             x_cod, x_scl = cod_x[c]
             for ih in halves:
                 n_cols = slice(ih * N_TILE, (ih + 1) * N_TILE)
-                for ot in range(O_TILES):
+                for ot in o_tiles:
                     m_cols = slice(ot * M_TILE, (ot + 1) * M_TILE)
                     nc.tensor.matmul_mx(
                         out=acc[(ot, ih)][:],
@@ -178,16 +177,23 @@ def tile_stebitlinear_t_kernel(tc, x, sign_weights, scales, grad_out, out):
         scalar_g(0, HEAD_VECTOR, OUT_F)
         first_x_regroup(nc.vector.tensor_copy, 0, 0, HEAD_VECTOR)
         first_x_regroup(nc.scalar.copy, 0, HEAD_VECTOR, N_TILE)
-        quantise_g(0)
+        quantise_g(0, 0, OUT_F)
         first_x_regroup(nc.vector.tensor_copy, 1, 0, HEAD_VECTOR)
         first_x_regroup(nc.scalar.copy, 1, HEAD_VECTOR, N_TILE)
         quantise_x(0, 0, N_TILE)
         passes(0, (0,))
 
-        for c in range(1, last):
-            if c + RAW_BUFS - 1 < CHUNKS:
-                load_g(c + RAW_BUFS - 1)
-                load_x(c + RAW_BUFS - 1)
+        for c in range(1, last - 1):
+            ahead = c + RAW_BUFS - 1
+            if ahead < last - 1:
+                load_g(ahead)
+                load_x(ahead)
+            elif ahead == last - 1:
+                load_x(last - 1)
+            elif ahead == last:
+                load_x(last)
+                load_g(last - 1)
+                load_g(last)
             if c == SCALES_LOADED:
                 load_scales()
             if c == SCALES_WIDENED:
@@ -202,24 +208,12 @@ def tile_stebitlinear_t_kernel(tc, x, sign_weights, scales, grad_out, out):
                 quantise_x(c - 1, 0, IN_F)
                 passes(c - 1, (0, 1))
             vector_x(c, X_SCALAR, IN_F)
-            quantise_g(c)
+            quantise_g(c, 0, OUT_F)
 
-        open_chunk(last)
-        quantise_x(last - 1, 0, IN_F)
-        passes(last - 1, (0, 1))
-        vector_g(last, 0, OUT_F)
-        scalar_x(last, 0, N_TILE)
-        quantise_x(last, 0, N_TILE)
-        quantise_g(last)
-        passes(last, (0,))
-        scalar_x(last, N_TILE, N_TILE + TAIL_SCALAR)
-        vector_x(last, N_TILE + TAIL_SCALAR, IN_F)
-        quantise_x(last, N_TILE, IN_F)
-        passes(last, (1,))
+        def o_cols(ot):
+            return ot * M_TILE, (ot + 1) * M_TILE
 
-        for bank, engine in OUT_ORDER:
-            ih = bank // O_TILES
-            ot = bank % O_TILES
+        def scale_out(ot, ih, engine):
             first = ot * GROUPS_PER_ROW + ih * GROUPS_PER_BANK
             scaled = res.tile([P, N_TILE], F32, name="scaled", tag="scaled")
             if engine == "v":
@@ -244,3 +238,29 @@ def tile_stebitlinear_t_kernel(tc, x, sign_weights, scales, grad_out, out):
                 out=out[ot * M_TILE : (ot + 1) * M_TILE, ih * N_TILE : (ih + 1) * N_TILE],
                 in_=scaled[:],
             )
+
+        open_chunk(last - 1)
+        open_chunk(last)
+        scalar_x(last - 1, 0, TAIL_X_SCALAR)
+        vector_x(last - 1, TAIL_X_SCALAR, IN_F)
+        quantise_x(last - 2, 0, IN_F)
+        passes(last - 2, (0, 1))
+        scalar_x(last, 0, TAIL_X_SCALAR)
+        vector_x(last, TAIL_X_SCALAR, IN_F)
+        quantise_x(last - 1, 0, IN_F)
+        scalar_g(last - 1, *o_cols(0))
+        vector_g(last, *o_cols(0))
+        quantise_x(last, 0, IN_F)
+        for ot in range(O_TILES):
+            if ot + 1 < O_TILES:
+                scalar_g(last - 1, *o_cols(ot + 1))
+                vector_g(last, *o_cols(ot + 1))
+            quantise_g(last - 1, *o_cols(ot))
+            quantise_g(last, *o_cols(ot))
+            passes(last - 1, (0, 1), (ot,))
+            passes(last, (0, 1), (ot,))
+            if ot > 0:
+                scale_out(ot - 1, 0, "s")
+                scale_out(ot - 1, 1, "v")
+        scale_out(O_TILES - 1, 0, "s")
+        scale_out(O_TILES - 1, 1, "v")

@@ -29,8 +29,10 @@ RAW_BUFS = 6
 SCALES_LOADED = 8
 SCALES_WIDENED = 11
 X_SCALAR = 736
+G_AHEAD = 1
 HEAD_VECTOR = 248
-TAIL_X_SCALAR = 512
+HEAD_X_VECTOR = 496
+TAIL_X_VECTOR = 288
 
 FLOPS = 2 * TOKENS * IN_F * OUT_F
 BYTES = 2 * TOKENS * (IN_F + OUT_F) + 2 * OUT_F * GROUPS_PER_ROW + 4 * OUT_F * IN_F
@@ -92,30 +94,15 @@ def tile_stebitlinear_t_kernel(tc, x, sign_weights, scales, grad_out, out):
             raw_x[c] = raw.tile([P, PACK, IN_F], BF16, name="x_raw", tag="x_raw")
             nc.sync.dma_start(out=raw_x[c][:], in_=xt[rows, :].rearrange("(p j) w -> p j w", j=PACK))
 
-        first_x = [
-            const.tile([P, PACK, N_TILE], BF16, name="first_x_%d" % ih) for ih in range(I_TILES)
-        ]
-
-        def load_first_x(ih):
-            cols = slice(ih * N_TILE, (ih + 1) * N_TILE)
-            nc.sync.dma_start(
-                out=first_x[ih][:], in_=xt[0:K_PASS, cols].rearrange("(p j) w -> p j w", j=PACK)
-            )
-
-        def first_x_regroup(copy, ih, lo, hi):
-            cols = slice(ih * N_TILE + lo, ih * N_TILE + hi)
-            copy(
-                out=grp_x[0][:, cols, :].rearrange("p (c i) t -> p c t i", i=RUN),
-                in_=first_x[ih][:, :, lo:hi].rearrange("p t (c i) -> p c t i", i=RUN),
-            )
-
-        def open_chunk(c):
+        def open_g(c):
             grp_g[c] = grp.tile([P, OUT_F, PACK], BF16, name="g_grp", tag="g_grp", align_bytes=64)
-            grp_x[c] = grp.tile([P, IN_F, PACK], BF16, name="x_grp", tag="x_grp", align_bytes=64)
             cod_g[c] = (
                 cod.tile([P, OUT_F], U32, name="g_cod", tag="g_cod", align_bytes=64),
                 cod.tile([P, OUT_F], U8, name="g_scl", tag="g_scl", align_bytes=64),
             )
+
+        def open_x(c):
+            grp_x[c] = grp.tile([P, IN_F, PACK], BF16, name="x_grp", tag="x_grp", align_bytes=64)
             cod_x[c] = (
                 cod.tile([P, IN_F], U32, name="x_cod", tag="x_cod", align_bytes=64),
                 cod.tile([P, IN_F], U8, name="x_scl", tag="x_scl", align_bytes=64),
@@ -166,52 +153,46 @@ def tile_stebitlinear_t_kernel(tc, x, sign_weights, scales, grad_out, out):
                         stop=(c == last),
                     )
 
-        load_g(0)
-        for ih in range(I_TILES):
-            load_first_x(ih)
-        for c in range(1, RAW_BUFS):
-            load_g(c)
+        def load_next(c):
+            if c + G_AHEAD < CHUNKS:
+                load_g(c + G_AHEAD)
             load_x(c)
-        open_chunk(0)
-        vector_g(0, 0, HEAD_VECTOR)
-        scalar_g(0, HEAD_VECTOR, OUT_F)
-        first_x_regroup(nc.vector.tensor_copy, 0, 0, HEAD_VECTOR)
-        first_x_regroup(nc.scalar.copy, 0, HEAD_VECTOR, N_TILE)
-        quantise_g(0, 0, OUT_F)
-        first_x_regroup(nc.vector.tensor_copy, 1, 0, HEAD_VECTOR)
-        first_x_regroup(nc.scalar.copy, 1, HEAD_VECTOR, N_TILE)
-        quantise_x(0, 0, N_TILE)
-        passes(0, (0,))
+
+        load_g(0)
+        for c in range(RAW_BUFS - G_AHEAD):
+            load_next(c)
+        for c in range(1 + G_AHEAD):
+            open_g(c)
+            vector_g(c, 0, HEAD_VECTOR)
+            scalar_g(c, HEAD_VECTOR, OUT_F)
+            if c > 0:
+                quantise_g(c - 1, 0, OUT_F)
+        quantise_g(G_AHEAD, 0, OUT_F)
+        open_x(0)
+        vector_x(0, 0, HEAD_X_VECTOR)
+        scalar_x(0, HEAD_X_VECTOR, IN_F)
 
         for c in range(1, last - 1):
-            ahead = c + RAW_BUFS - 1
-            if ahead < last - 1:
-                load_g(ahead)
-                load_x(ahead)
-            elif ahead == last - 1:
-                load_x(last - 1)
-            elif ahead == last:
-                load_x(last)
-                load_g(last - 1)
-                load_g(last)
+            ahead = c + RAW_BUFS - G_AHEAD - 1
+            if ahead < CHUNKS:
+                load_next(ahead)
             if c == SCALES_LOADED:
                 load_scales()
             if c == SCALES_WIDENED:
                 widen_scales()
-            open_chunk(c)
-            vector_g(c, 0, OUT_F)
+            open_x(c)
             scalar_x(c, 0, X_SCALAR)
-            if c == 1:
-                quantise_x(0, N_TILE, IN_F)
-                passes(0, (1,))
-            else:
-                quantise_x(c - 1, 0, IN_F)
-                passes(c - 1, (0, 1))
+            if c + G_AHEAD < last - 1:
+                open_g(c + G_AHEAD)
+                vector_g(c + G_AHEAD, 0, OUT_F)
+            quantise_x(c - 1, 0, IN_F)
+            passes(c - 1, (0, 1))
             vector_x(c, X_SCALAR, IN_F)
-            quantise_g(c, 0, OUT_F)
+            if c + G_AHEAD < last - 1:
+                quantise_g(c + G_AHEAD, 0, OUT_F)
 
-        def o_cols(ot):
-            return ot * M_TILE, (ot + 1) * M_TILE
+        pair = (last - 1, last)
+        half_g = OUT_F // 2
 
         def scale_out(ot, ih, engine):
             first = ot * GROUPS_PER_ROW + ih * GROUPS_PER_BANK
@@ -239,28 +220,43 @@ def tile_stebitlinear_t_kernel(tc, x, sign_weights, scales, grad_out, out):
                 in_=scaled[:],
             )
 
-        open_chunk(last - 1)
-        open_chunk(last)
-        scalar_x(last - 1, 0, TAIL_X_SCALAR)
-        vector_x(last - 1, TAIL_X_SCALAR, IN_F)
+        def store_step(o_tiles, halves):
+            engines = ("s", "v")
+            for k, (ot, ih) in enumerate([(ot, ih) for ot in o_tiles for ih in halves]):
+                scale_out(ot, ih, engines[k])
+
+        for c in pair:
+            open_g(c)
+            open_x(c)
+
+        scalar_x(last - 1, 0, N_TILE)
+        vector_g(last - 1, 0, half_g)
+        vector_g(last, 0, half_g)
+        scalar_x(last, TAIL_X_VECTOR, N_TILE)
         quantise_x(last - 2, 0, IN_F)
         passes(last - 2, (0, 1))
-        scalar_x(last, 0, TAIL_X_SCALAR)
-        vector_x(last, TAIL_X_SCALAR, IN_F)
-        quantise_x(last - 1, 0, IN_F)
-        scalar_g(last - 1, *o_cols(0))
-        vector_g(last, *o_cols(0))
-        quantise_x(last, 0, IN_F)
-        for ot in range(O_TILES):
-            if ot + 1 < O_TILES:
-                scalar_g(last - 1, *o_cols(ot + 1))
-                vector_g(last, *o_cols(ot + 1))
-            quantise_g(last - 1, *o_cols(ot))
-            quantise_g(last, *o_cols(ot))
-            passes(last - 1, (0, 1), (ot,))
-            passes(last, (0, 1), (ot,))
-            if ot > 0:
-                scale_out(ot - 1, 0, "s")
-                scale_out(ot - 1, 1, "v")
-        scale_out(O_TILES - 1, 0, "s")
-        scale_out(O_TILES - 1, 1, "v")
+        vector_x(last, 0, TAIL_X_VECTOR)
+        for c in pair:
+            quantise_g(c, 0, half_g)
+        scalar_x(last - 1, N_TILE, IN_F)
+        vector_x(last, N_TILE, IN_F)
+        for c in pair:
+            quantise_x(c, 0, N_TILE)
+            passes(c, (0,), (0, 1))
+        scalar_g(last - 1, half_g, half_g + M_TILE)
+        vector_g(last, half_g, half_g + M_TILE)
+        for c in pair:
+            quantise_x(c, N_TILE, IN_F)
+            passes(c, (1,), (0, 1))
+        store_step((0, 1), (0,))
+        scalar_g(last - 1, half_g + M_TILE, OUT_F)
+        vector_g(last, half_g + M_TILE, OUT_F)
+        for c in pair:
+            quantise_g(c, half_g, half_g + M_TILE)
+            passes(c, (0, 1), (2,))
+        store_step((0, 1), (1,))
+        for c in pair:
+            quantise_g(c, half_g + M_TILE, OUT_F)
+            passes(c, (0, 1), (3,))
+        store_step((2,), (0, 1))
+        store_step((3,), (0, 1))

@@ -1,6 +1,7 @@
 from contextlib import ExitStack
 
 import concourse.mybir as mybir
+from concourse.masks import make_identity
 
 BF16 = mybir.dt.bfloat16
 F32 = mybir.dt.float32
@@ -26,13 +27,19 @@ GROUPS_PER_BANK = N_TILE // GROUP
 RUN = 4
 
 RAW_BUFS = 6
+RELAYED = range(1, 12)
+RELAY_COLS = 256
+RELAY_X_VECTOR = 424
+BANKS = [(ot, ih) for ih in range(I_TILES) for ot in range(O_TILES)]
+LATE_BANK = BANKS[-1]
+EARLY_BANKS = BANKS[:-1]
+LEFT_BANKS = BANKS[:O_TILES]
+RIGHT_BANKS = BANKS[O_TILES:]
+LATE_PASSES = 5
 SCALES_LOADED = 8
 SCALES_WIDENED = 11
-X_SCALAR = 736
-G_AHEAD = 1
-HEAD_VECTOR = 248
-HEAD_X_VECTOR = 496
-TAIL_X_VECTOR = 288
+G_VECTOR = 248
+X_VECTOR = 528
 
 FLOPS = 2 * TOKENS * IN_F * OUT_F
 BYTES = 2 * TOKENS * (IN_F + OUT_F) + 2 * OUT_F * GROUPS_PER_ROW + 4 * OUT_F * IN_F
@@ -55,7 +62,7 @@ def tile_stebitlinear_t_kernel(tc, x, sign_weights, scales, grad_out, out):
         const = ctx.enter_context(tc.tile_pool(name="const", bufs=1))
         raw = ctx.enter_context(tc.tile_pool(name="raw", bufs=RAW_BUFS))
         grp = ctx.enter_context(tc.tile_pool(name="grp", bufs=3))
-        cod = ctx.enter_context(tc.tile_pool(name="cod", bufs=3))
+        cod = ctx.enter_context(tc.tile_pool(name="cod", bufs=RELAYED.stop + 2))
         res = ctx.enter_context(tc.tile_pool(name="res", bufs=O_TILES * I_TILES))
         psum = ctx.enter_context(tc.psum_pool(name="psum", bufs=1))
         ctx.enter_context(tc.manual_schedule())
@@ -79,10 +86,38 @@ def tile_stebitlinear_t_kernel(tc, x, sign_weights, scales, grad_out, out):
         def widen_scales():
             nc.scalar.activation(out=sc32[:], in_=sc_bf[:], func=mybir.ActivationFunctionType.Copy)
 
+        ident = const.tile([P, P], BF16, name="ident")
+        make_identity(nc, ident[:])
+
         acc = {}
-        for ih in range(I_TILES):
-            for ot in range(O_TILES):
-                acc[(ot, ih)] = psum.tile([P, N_TILE], F32, name="acc_%d_%d" % (ot, ih))
+
+        def open_bank(ot, ih):
+            acc[(ot, ih)] = psum.tile([P, N_TILE], F32, name="acc", tag="acc_%d_%d" % (ot, ih))
+
+        for ot, ih in EARLY_BANKS:
+            open_bank(ot, ih)
+
+        relay = {}
+
+        def relay_fill(c):
+            relay[c] = psum.tile(
+                [P, RELAY_COLS, PACK], BF16, name="relay", tag="acc_%d_%d" % LATE_BANK
+            )
+            half = RELAY_COLS // 2
+            for lo in (0, half):
+                nc.tensor.matmul(
+                    out=relay[c][:, lo : lo + half, :].rearrange("p w t -> p t w"),
+                    lhsT=ident[:],
+                    rhs=raw_x[c][:, :, lo : lo + half],
+                    start=True,
+                    stop=True,
+                )
+
+        def relay_copy(c):
+            nc.scalar.copy(
+                out=grp_x[c][:, 0:RELAY_COLS, :].rearrange("p w t -> p (w t)"),
+                in_=relay[c][:].rearrange("p w t -> p (w t)"),
+            )
 
         def load_g(c):
             rows = slice(c * K_PASS, (c + 1) * K_PASS)
@@ -93,6 +128,23 @@ def tile_stebitlinear_t_kernel(tc, x, sign_weights, scales, grad_out, out):
             rows = slice(c * K_PASS, (c + 1) * K_PASS)
             raw_x[c] = raw.tile([P, PACK, IN_F], BF16, name="x_raw", tag="x_raw")
             nc.sync.dma_start(out=raw_x[c][:], in_=xt[rows, :].rearrange("(p j) w -> p j w", j=PACK))
+
+        half_x = {}
+
+        def load_half_x(ih):
+            rows = slice(last * K_PASS, (last + 1) * K_PASS)
+            cols = slice(ih * N_TILE, (ih + 1) * N_TILE)
+            half_x[ih] = const.tile([P, PACK, N_TILE], BF16, name="half_x_%d" % ih)
+            nc.sync.dma_start(
+                out=half_x[ih][:], in_=xt[rows, cols].rearrange("(p j) w -> p j w", j=PACK)
+            )
+
+        def regroup_half_x(copy, ih, lo, hi):
+            cols = slice(ih * N_TILE + lo, ih * N_TILE + hi)
+            copy(
+                out=grp_x[last][:, cols, :].rearrange("p (c i) t -> p c t i", i=RUN),
+                in_=half_x[ih][:, :, lo:hi].rearrange("p t (c i) -> p c t i", i=RUN),
+            )
 
         def open_g(c):
             grp_g[c] = grp.tile([P, OUT_F, PACK], BF16, name="g_grp", tag="g_grp", align_bytes=64)
@@ -136,63 +188,70 @@ def tile_stebitlinear_t_kernel(tc, x, sign_weights, scales, grad_out, out):
                 in_=grp_x[c][:, lo:hi, :].rearrange("p w j -> p (w j)"),
             )
 
-        def passes(c, halves, o_tiles=range(O_TILES)):
+        def passes(c, banks):
             g_cod, g_scl = cod_g[c]
             x_cod, x_scl = cod_x[c]
-            for ih in halves:
+            for ot, ih in banks:
+                m_cols = slice(ot * M_TILE, (ot + 1) * M_TILE)
                 n_cols = slice(ih * N_TILE, (ih + 1) * N_TILE)
-                for ot in o_tiles:
-                    m_cols = slice(ot * M_TILE, (ot + 1) * M_TILE)
-                    nc.tensor.matmul_mx(
-                        out=acc[(ot, ih)][:],
-                        lhsT=g_cod[:, m_cols].bitcast(E5M2X4),
-                        lhsT_scale=g_scl[:, m_cols],
-                        rhs=x_cod[:, n_cols].bitcast(E4M3X4),
-                        rhs_scale=x_scl[:, n_cols],
-                        start=(c == 0),
-                        stop=(c == last),
-                    )
+                nc.tensor.matmul_mx(
+                    out=acc[(ot, ih)][:],
+                    lhsT=g_cod[:, m_cols].bitcast(E5M2X4),
+                    lhsT_scale=g_scl[:, m_cols],
+                    rhs=x_cod[:, n_cols].bitcast(E4M3X4),
+                    rhs_scale=x_scl[:, n_cols],
+                    start=(c == 0),
+                    stop=(c == last),
+                )
 
-        def load_next(c):
-            if c + G_AHEAD < CHUNKS:
-                load_g(c + G_AHEAD)
-            load_x(c)
+        late = list(range(last - 1))
 
-        load_g(0)
-        for c in range(RAW_BUFS - G_AHEAD):
-            load_next(c)
-        for c in range(1 + G_AHEAD):
-            open_g(c)
-            vector_g(c, 0, HEAD_VECTOR)
-            scalar_g(c, HEAD_VECTOR, OUT_F)
+        def catch_up(c, count):
+            if LATE_BANK not in acc:
+                open_bank(*LATE_BANK)
+            for k in late[:count]:
+                if k < c:
+                    passes(k, (LATE_BANK,))
+                    late.remove(k)
+
+        def load(c):
+            if c < last:
+                load_g(c)
+                load_x(c)
+            elif c == last:
+                load_half_x(0)
+                load_g(c)
+                load_half_x(1)
+
+        for c in range(RAW_BUFS):
+            load(c)
+        for c in range(last):
+            ahead = c + RAW_BUFS - 1
             if c > 0:
-                quantise_g(c - 1, 0, OUT_F)
-        quantise_g(G_AHEAD, 0, OUT_F)
-        open_x(0)
-        vector_x(0, 0, HEAD_X_VECTOR)
-        scalar_x(0, HEAD_X_VECTOR, IN_F)
-
-        for c in range(1, last - 1):
-            ahead = c + RAW_BUFS - G_AHEAD - 1
-            if ahead < CHUNKS:
-                load_next(ahead)
+                load(ahead)
             if c == SCALES_LOADED:
                 load_scales()
             if c == SCALES_WIDENED:
                 widen_scales()
+            open_g(c)
             open_x(c)
-            scalar_x(c, 0, X_SCALAR)
-            if c + G_AHEAD < last - 1:
-                open_g(c + G_AHEAD)
-                vector_g(c + G_AHEAD, 0, OUT_F)
-            quantise_x(c - 1, 0, IN_F)
-            passes(c - 1, (0, 1))
-            vector_x(c, X_SCALAR, IN_F)
-            if c + G_AHEAD < last - 1:
-                quantise_g(c + G_AHEAD, 0, OUT_F)
-
-        pair = (last - 1, last)
-        half_g = OUT_F // 2
+            if c in RELAYED:
+                relay_fill(c)
+            vector_g(c, 0, G_VECTOR)
+            scalar_g(c, G_VECTOR, OUT_F)
+            if c > 0:
+                quantise_x(c - 1, 0, IN_F)
+                passes(c - 1, EARLY_BANKS)
+                if c >= RELAYED.stop:
+                    catch_up(c, LATE_PASSES)
+            if c in RELAYED:
+                vector_x(c, RELAY_COLS, RELAY_COLS + RELAY_X_VECTOR)
+                scalar_x(c, RELAY_COLS + RELAY_X_VECTOR, IN_F)
+                relay_copy(c)
+            else:
+                vector_x(c, 0, X_VECTOR)
+                scalar_x(c, X_VECTOR, IN_F)
+            quantise_g(c, 0, OUT_F)
 
         def scale_out(ot, ih, engine):
             first = ot * GROUPS_PER_ROW + ih * GROUPS_PER_BANK
@@ -220,43 +279,27 @@ def tile_stebitlinear_t_kernel(tc, x, sign_weights, scales, grad_out, out):
                 in_=scaled[:],
             )
 
-        def store_step(o_tiles, halves):
-            engines = ("s", "v")
-            for k, (ot, ih) in enumerate([(ot, ih) for ot in o_tiles for ih in halves]):
-                scale_out(ot, ih, engines[k])
-
-        for c in pair:
-            open_g(c)
-            open_x(c)
-
-        scalar_x(last - 1, 0, N_TILE)
-        vector_g(last - 1, 0, half_g)
-        vector_g(last, 0, half_g)
-        scalar_x(last, TAIL_X_VECTOR, N_TILE)
-        quantise_x(last - 2, 0, IN_F)
-        passes(last - 2, (0, 1))
-        vector_x(last, 0, TAIL_X_VECTOR)
-        for c in pair:
-            quantise_g(c, 0, half_g)
-        scalar_x(last - 1, N_TILE, IN_F)
-        vector_x(last, N_TILE, IN_F)
-        for c in pair:
-            quantise_x(c, 0, N_TILE)
-            passes(c, (0,), (0, 1))
-        scalar_g(last - 1, half_g, half_g + M_TILE)
-        vector_g(last, half_g, half_g + M_TILE)
-        for c in pair:
-            quantise_x(c, N_TILE, IN_F)
-            passes(c, (1,), (0, 1))
-        store_step((0, 1), (0,))
-        scalar_g(last - 1, half_g + M_TILE, OUT_F)
-        vector_g(last, half_g + M_TILE, OUT_F)
-        for c in pair:
-            quantise_g(c, half_g, half_g + M_TILE)
-            passes(c, (0, 1), (2,))
-        store_step((0, 1), (1,))
-        for c in pair:
-            quantise_g(c, half_g + M_TILE, OUT_F)
-            passes(c, (0, 1), (3,))
-        store_step((2,), (0, 1))
-        store_step((3,), (0, 1))
+        open_g(last)
+        open_x(last)
+        vector_g(last, 0, 248)
+        scalar_g(last, 248, OUT_F)
+        regroup_half_x(nc.vector.tensor_copy, 0, 0, 264)
+        regroup_half_x(nc.scalar.copy, 0, 264, N_TILE)
+        quantise_x(last - 1, 0, N_TILE)
+        passes(last - 1, LEFT_BANKS)
+        quantise_g(last, 0, OUT_F)
+        regroup_half_x(nc.vector.tensor_copy, 1, 0, 264)
+        regroup_half_x(nc.scalar.copy, 1, 264, N_TILE)
+        quantise_x(last, 0, N_TILE)
+        passes(last, LEFT_BANKS)
+        scale_out(0, 0, "s")
+        quantise_x(last - 1, N_TILE, IN_F)
+        quantise_x(last, N_TILE, IN_F)
+        catch_up(last - 1, CHUNKS)
+        passes(last - 1, RIGHT_BANKS)
+        passes(last, RIGHT_BANKS)
+        scale_out(1, 0, "v")
+        scale_out(2, 0, "s")
+        scale_out(3, 0, "v")
+        for ot in range(O_TILES):
+            scale_out(ot, 1, "sv"[ot % 2])

@@ -27,9 +27,9 @@ GROUPS_PER_BANK = N_TILE // GROUP
 RUN = 4
 
 RAW_BUFS = 6
-RELAYED = range(1, 12)
+RELAYED = range(1, 11)
 RELAY_COLS = 256
-RELAY_X_VECTOR = 424
+RELAY_X_VECTOR = 440
 BANKS = [(ot, ih) for ih in range(I_TILES) for ot in range(O_TILES)]
 LATE_BANK = BANKS[-1]
 EARLY_BANKS = BANKS[:-1]
@@ -38,7 +38,8 @@ RIGHT_BANKS = BANKS[O_TILES:]
 LATE_PASSES = 5
 SCALES_LOADED = 8
 SCALES_WIDENED = 11
-G_VECTOR = 248
+G_VECTOR = 264
+HALF_X_VECTOR = 264
 X_VECTOR = 528
 
 FLOPS = 2 * TOKENS * IN_F * OUT_F
@@ -57,6 +58,7 @@ def tile_stebitlinear_t_kernel(tc, x, sign_weights, scales, grad_out, out):
     xt = x.flatten_outer_dims()
     gt = grad_out.flatten_outer_dims()
     last = CHUNKS - 1
+    pair = (last - 1, last)
 
     with ExitStack() as ctx:
         const = ctx.enter_context(tc.tile_pool(name="const", bufs=1))
@@ -129,22 +131,25 @@ def tile_stebitlinear_t_kernel(tc, x, sign_weights, scales, grad_out, out):
             raw_x[c] = raw.tile([P, PACK, IN_F], BF16, name="x_raw", tag="x_raw")
             nc.sync.dma_start(out=raw_x[c][:], in_=xt[rows, :].rearrange("(p j) w -> p j w", j=PACK))
 
-        half_x = {}
-
-        def load_half_x(ih):
-            rows = slice(last * K_PASS, (last + 1) * K_PASS)
+        def load_half_x(c, ih):
+            rows = slice(c * K_PASS, (c + 1) * K_PASS)
             cols = slice(ih * N_TILE, (ih + 1) * N_TILE)
-            half_x[ih] = const.tile([P, PACK, N_TILE], BF16, name="half_x_%d" % ih)
+            if ih == 0:
+                raw_x[c] = raw.tile([P, I_TILES, PACK, N_TILE], BF16, name="x_raw", tag="x_raw")
             nc.sync.dma_start(
-                out=half_x[ih][:], in_=xt[rows, cols].rearrange("(p j) w -> p j w", j=PACK)
+                out=raw_x[c][:, ih, :, :], in_=xt[rows, cols].rearrange("(p j) w -> p j w", j=PACK)
             )
 
-        def regroup_half_x(copy, ih, lo, hi):
-            cols = slice(ih * N_TILE + lo, ih * N_TILE + hi)
-            copy(
-                out=grp_x[last][:, cols, :].rearrange("p (c i) t -> p c t i", i=RUN),
-                in_=half_x[ih][:, :, lo:hi].rearrange("p t (c i) -> p c t i", i=RUN),
-            )
+        def regroup_half_x(c, ih):
+            for copy, lo, hi in (
+                (nc.vector.tensor_copy, 0, HALF_X_VECTOR),
+                (nc.scalar.copy, HALF_X_VECTOR, N_TILE),
+            ):
+                cols = slice(ih * N_TILE + lo, ih * N_TILE + hi)
+                copy(
+                    out=grp_x[c][:, cols, :].rearrange("p (c i) t -> p c t i", i=RUN),
+                    in_=raw_x[c][:, ih, :, lo:hi].rearrange("p t (c i) -> p c t i", i=RUN),
+                )
 
         def open_g(c):
             grp_g[c] = grp.tile([P, OUT_F, PACK], BF16, name="g_grp", tag="g_grp", align_bytes=64)
@@ -215,31 +220,38 @@ def tile_stebitlinear_t_kernel(tc, x, sign_weights, scales, grad_out, out):
                     late.remove(k)
 
         def load(c):
-            if c < last:
-                load_g(c)
+            if c + 1 < CHUNKS and c <= pair[0]:
+                load_g(c + 1)
+            if c < pair[0]:
                 load_x(c)
-            elif c == last:
-                load_half_x(0)
-                load_g(c)
-                load_half_x(1)
+            elif c == pair[0]:
+                for ih in range(I_TILES):
+                    for k in pair:
+                        load_half_x(k, ih)
 
-        for c in range(RAW_BUFS):
+        def regroup_g(c):
+            open_g(c)
+            vector_g(c, 0, G_VECTOR)
+            scalar_g(c, G_VECTOR, OUT_F)
+
+        load_g(0)
+        for c in range(RAW_BUFS - 1):
             load(c)
-        for c in range(last):
-            ahead = c + RAW_BUFS - 1
+        regroup_g(0)
+        for c in range(pair[0]):
             if c > 0:
-                load(ahead)
+                load(c + RAW_BUFS - 2)
             if c == SCALES_LOADED:
                 load_scales()
             if c == SCALES_WIDENED:
                 widen_scales()
-            open_g(c)
             open_x(c)
             if c in RELAYED:
                 relay_fill(c)
-            vector_g(c, 0, G_VECTOR)
-            scalar_g(c, G_VECTOR, OUT_F)
-            if c > 0:
+            regroup_g(c + 1)
+            if c == 0:
+                quantise_g(0, 0, OUT_F)
+            else:
                 quantise_x(c - 1, 0, IN_F)
                 passes(c - 1, EARLY_BANKS)
                 if c >= RELAYED.stop:
@@ -251,7 +263,7 @@ def tile_stebitlinear_t_kernel(tc, x, sign_weights, scales, grad_out, out):
             else:
                 vector_x(c, 0, X_VECTOR)
                 scalar_x(c, X_VECTOR, IN_F)
-            quantise_g(c, 0, OUT_F)
+            quantise_g(c + 1, 0, OUT_F)
 
         def scale_out(ot, ih, engine):
             first = ot * GROUPS_PER_ROW + ih * GROUPS_PER_BANK
@@ -279,26 +291,27 @@ def tile_stebitlinear_t_kernel(tc, x, sign_weights, scales, grad_out, out):
                 in_=scaled[:],
             )
 
-        open_g(last)
-        open_x(last)
-        vector_g(last, 0, 248)
-        scalar_g(last, 248, OUT_F)
-        regroup_half_x(nc.vector.tensor_copy, 0, 0, 264)
-        regroup_half_x(nc.scalar.copy, 0, 264, N_TILE)
+        for c in pair:
+            open_x(c)
+        regroup_g(last)
+        quantise_x(last - 2, 0, IN_F)
+        passes(last - 2, EARLY_BANKS)
+        catch_up(last - 1, CHUNKS)
+        regroup_half_x(last - 1, 0)
+        quantise_g(last, 0, OUT_F)
+        regroup_half_x(last, 0)
         quantise_x(last - 1, 0, N_TILE)
         passes(last - 1, LEFT_BANKS)
-        quantise_g(last, 0, OUT_F)
-        regroup_half_x(nc.vector.tensor_copy, 1, 0, 264)
-        regroup_half_x(nc.scalar.copy, 1, 264, N_TILE)
+        regroup_half_x(last - 1, 1)
         quantise_x(last, 0, N_TILE)
         passes(last, LEFT_BANKS)
-        scale_out(0, 0, "s")
+        regroup_half_x(last, 1)
         quantise_x(last - 1, N_TILE, IN_F)
-        quantise_x(last, N_TILE, IN_F)
-        catch_up(last - 1, CHUNKS)
         passes(last - 1, RIGHT_BANKS)
-        passes(last, RIGHT_BANKS)
+        scale_out(0, 0, "s")
         scale_out(1, 0, "v")
+        quantise_x(last, N_TILE, IN_F)
+        passes(last, RIGHT_BANKS)
         scale_out(2, 0, "s")
         scale_out(3, 0, "v")
         for ot in range(O_TILES):

@@ -27,7 +27,7 @@ GROUPS_PER_BANK = N_TILE // GROUP
 RUN = 4
 
 RAW_BUFS = 6
-RELAYED = range(1, 11)
+RELAYED = range(0, 0)
 RELAY_COLS = 256
 RELAY_X_VECTOR = 440
 BANKS = [(ot, ih) for ih in range(I_TILES) for ot in range(O_TILES)]
@@ -64,7 +64,7 @@ def tile_stebitlinear_t_kernel(tc, x, sign_weights, scales, grad_out, out):
         const = ctx.enter_context(tc.tile_pool(name="const", bufs=1))
         raw = ctx.enter_context(tc.tile_pool(name="raw", bufs=RAW_BUFS))
         grp = ctx.enter_context(tc.tile_pool(name="grp", bufs=3))
-        cod = ctx.enter_context(tc.tile_pool(name="cod", bufs=RELAYED.stop + 2))
+        cod = ctx.enter_context(tc.tile_pool(name="cod", bufs=4))
         res = ctx.enter_context(tc.tile_pool(name="res", bufs=O_TILES * I_TILES))
         psum = ctx.enter_context(tc.psum_pool(name="psum", bufs=1))
         ctx.enter_context(tc.manual_schedule())

@@ -38,9 +38,9 @@ RIGHT_BANKS = BANKS[O_TILES:]
 LATE_PASSES = 5
 SCALES_LOADED = 8
 SCALES_WIDENED = 11
-G_VECTOR = 264
-HALF_X_VECTOR = 264
-X_VECTOR = 528
+G_VECTOR = 248
+HALF_X_VECTOR = 248
+X_VECTOR = 512
 
 FLOPS = 2 * TOKENS * IN_F * OUT_F
 BYTES = 2 * TOKENS * (IN_F + OUT_F) + 2 * OUT_F * GROUPS_PER_ROW + 4 * OUT_F * IN_F

@@ -1,7 +1,6 @@
 from contextlib import ExitStack
 
 import concourse.mybir as mybir
-from concourse.masks import make_identity
 
 BF16 = mybir.dt.bfloat16
 F32 = mybir.dt.float32
@@ -27,30 +26,14 @@ GROUPS_PER_BANK = N_TILE // GROUP
 RUN = 4
 
 RAW_BUFS = 6
-RELAYED = range(0, 0)
-RELAY_COLS = 256
-RELAY_X_VECTOR = 440
-BANKS = [(ot, ih) for ih in range(I_TILES) for ot in range(O_TILES)]
-LATE_BANK = BANKS[-1]
-EARLY_BANKS = BANKS[:-1]
-LEFT_BANKS = BANKS[:O_TILES]
-RIGHT_BANKS = BANKS[O_TILES:]
-LATE_PASSES = 5
+G_VECTOR = 248
+X_VECTOR = 512
+HALF_X_VECTOR = 248
 SCALES_LOADED = 8
 SCALES_WIDENED = 11
-G_VECTOR = 248
-HALF_X_VECTOR = 248
-X_VECTOR = 512
 
 FLOPS = 2 * TOKENS * IN_F * OUT_F
 BYTES = 2 * TOKENS * (IN_F + OUT_F) + 2 * OUT_F * GROUPS_PER_ROW + 4 * OUT_F * IN_F
-
-
-def regroup(copy, dst, src, lo, hi):
-    copy(
-        out=dst[:, lo:hi, :].rearrange("p (c i) t -> p c t i", i=RUN),
-        in_=src[:, :, lo:hi].rearrange("p t (c i) -> p c t i", i=RUN),
-    )
 
 
 def tile_stebitlinear_t_kernel(tc, x, sign_weights, scales, grad_out, out):
@@ -59,6 +42,7 @@ def tile_stebitlinear_t_kernel(tc, x, sign_weights, scales, grad_out, out):
     gt = grad_out.flatten_outer_dims()
     last = CHUNKS - 1
     pair = (last - 1, last)
+    left, right = range(I_TILES)
 
     with ExitStack() as ctx:
         const = ctx.enter_context(tc.tile_pool(name="const", bufs=1))
@@ -88,38 +72,10 @@ def tile_stebitlinear_t_kernel(tc, x, sign_weights, scales, grad_out, out):
         def widen_scales():
             nc.scalar.activation(out=sc32[:], in_=sc_bf[:], func=mybir.ActivationFunctionType.Copy)
 
-        ident = const.tile([P, P], BF16, name="ident")
-        make_identity(nc, ident[:])
-
         acc = {}
-
-        def open_bank(ot, ih):
-            acc[(ot, ih)] = psum.tile([P, N_TILE], F32, name="acc", tag="acc_%d_%d" % (ot, ih))
-
-        for ot, ih in EARLY_BANKS:
-            open_bank(ot, ih)
-
-        relay = {}
-
-        def relay_fill(c):
-            relay[c] = psum.tile(
-                [P, RELAY_COLS, PACK], BF16, name="relay", tag="acc_%d_%d" % LATE_BANK
-            )
-            half = RELAY_COLS // 2
-            for lo in (0, half):
-                nc.tensor.matmul(
-                    out=relay[c][:, lo : lo + half, :].rearrange("p w t -> p t w"),
-                    lhsT=ident[:],
-                    rhs=raw_x[c][:, :, lo : lo + half],
-                    start=True,
-                    stop=True,
-                )
-
-        def relay_copy(c):
-            nc.scalar.copy(
-                out=grp_x[c][:, 0:RELAY_COLS, :].rearrange("p w t -> p (w t)"),
-                in_=relay[c][:].rearrange("p w t -> p (w t)"),
-            )
+        for ih in range(I_TILES):
+            for ot in range(O_TILES):
+                acc[(ot, ih)] = psum.tile([P, N_TILE], F32, name="acc_%d_%d" % (ot, ih))
 
         def load_g(c):
             rows = slice(c * K_PASS, (c + 1) * K_PASS)
@@ -131,32 +87,29 @@ def tile_stebitlinear_t_kernel(tc, x, sign_weights, scales, grad_out, out):
             raw_x[c] = raw.tile([P, PACK, IN_F], BF16, name="x_raw", tag="x_raw")
             nc.sync.dma_start(out=raw_x[c][:], in_=xt[rows, :].rearrange("(p j) w -> p j w", j=PACK))
 
-        def load_half_x(c, ih):
-            rows = slice(c * K_PASS, (c + 1) * K_PASS)
-            cols = slice(ih * N_TILE, (ih + 1) * N_TILE)
-            if ih == 0:
-                raw_x[c] = raw.tile([P, I_TILES, PACK, N_TILE], BF16, name="x_raw", tag="x_raw")
-            nc.sync.dma_start(
-                out=raw_x[c][:, ih, :, :], in_=xt[rows, cols].rearrange("(p j) w -> p j w", j=PACK)
-            )
+        def load(c):
+            if c + 1 < CHUNKS:
+                load_g(c + 1)
+            if c < CHUNKS:
+                load_x(c)
 
-        def regroup_half_x(c, ih):
+        def regroup(dst, src, at, v_cols, width):
             for copy, lo, hi in (
-                (nc.vector.tensor_copy, 0, HALF_X_VECTOR),
-                (nc.scalar.copy, HALF_X_VECTOR, N_TILE),
+                (nc.vector.tensor_copy, 0, v_cols),
+                (nc.scalar.copy, v_cols, width),
             ):
-                cols = slice(ih * N_TILE + lo, ih * N_TILE + hi)
                 copy(
-                    out=grp_x[c][:, cols, :].rearrange("p (c i) t -> p c t i", i=RUN),
-                    in_=raw_x[c][:, ih, :, lo:hi].rearrange("p t (c i) -> p c t i", i=RUN),
+                    out=dst[:, at + lo : at + hi, :].rearrange("p (c i) t -> p c t i", i=RUN),
+                    in_=src[:, :, lo:hi].rearrange("p t (c i) -> p c t i", i=RUN),
                 )
 
-        def open_g(c):
+        def regroup_g(c):
             grp_g[c] = grp.tile([P, OUT_F, PACK], BF16, name="g_grp", tag="g_grp", align_bytes=64)
             cod_g[c] = (
                 cod.tile([P, OUT_F], U32, name="g_cod", tag="g_cod", align_bytes=64),
                 cod.tile([P, OUT_F], U8, name="g_scl", tag="g_scl", align_bytes=64),
             )
+            regroup(grp_g[c], raw_g[c], 0, G_VECTOR, OUT_F)
 
         def open_x(c):
             grp_x[c] = grp.tile([P, IN_F, PACK], BF16, name="x_grp", tag="x_grp", align_bytes=64)
@@ -165,24 +118,20 @@ def tile_stebitlinear_t_kernel(tc, x, sign_weights, scales, grad_out, out):
                 cod.tile([P, IN_F], U8, name="x_scl", tag="x_scl", align_bytes=64),
             )
 
-        def vector_g(c, lo, hi):
-            regroup(nc.vector.tensor_copy, grp_g[c], raw_g[c], lo, hi)
+        def regroup_x(c):
+            open_x(c)
+            regroup(grp_x[c], raw_x[c], 0, X_VECTOR, IN_F)
 
-        def scalar_g(c, lo, hi):
-            regroup(nc.scalar.copy, grp_g[c], raw_g[c], lo, hi)
+        def regroup_half_x(c, ih):
+            at = ih * N_TILE
+            regroup(grp_x[c], raw_x[c][:, :, at : at + N_TILE], at, HALF_X_VECTOR, N_TILE)
 
-        def vector_x(c, lo, hi):
-            regroup(nc.vector.tensor_copy, grp_x[c], raw_x[c], lo, hi)
-
-        def scalar_x(c, lo, hi):
-            regroup(nc.scalar.copy, grp_x[c], raw_x[c], lo, hi)
-
-        def quantise_g(c, lo, hi):
+        def quantise_g(c):
             g_cod, g_scl = cod_g[c]
             nc.vector.quantize_mx(
-                out=g_cod[:, lo:hi].bitcast(E5M2X4),
-                scales=g_scl[:, lo:hi],
-                in_=grp_g[c][:, lo:hi, :].rearrange("p w j -> p (w j)"),
+                out=g_cod[:].bitcast(E5M2X4),
+                scales=g_scl[:],
+                in_=grp_g[c][:].rearrange("p w j -> p (w j)"),
             )
 
         def quantise_x(c, lo, hi):
@@ -193,12 +142,12 @@ def tile_stebitlinear_t_kernel(tc, x, sign_weights, scales, grad_out, out):
                 in_=grp_x[c][:, lo:hi, :].rearrange("p w j -> p (w j)"),
             )
 
-        def passes(c, banks):
+        def passes(c, ih):
             g_cod, g_scl = cod_g[c]
             x_cod, x_scl = cod_x[c]
-            for ot, ih in banks:
+            n_cols = slice(ih * N_TILE, (ih + 1) * N_TILE)
+            for ot in range(O_TILES):
                 m_cols = slice(ot * M_TILE, (ot + 1) * M_TILE)
-                n_cols = slice(ih * N_TILE, (ih + 1) * N_TILE)
                 nc.tensor.matmul_mx(
                     out=acc[(ot, ih)][:],
                     lhsT=g_cod[:, m_cols].bitcast(E5M2X4),
@@ -209,66 +158,19 @@ def tile_stebitlinear_t_kernel(tc, x, sign_weights, scales, grad_out, out):
                     stop=(c == last),
                 )
 
-        late = list(range(last - 1))
+        def multiply(c):
+            quantise_x(c, 0, IN_F)
+            for ih in range(I_TILES):
+                passes(c, ih)
 
-        def catch_up(c, count):
-            if LATE_BANK not in acc:
-                open_bank(*LATE_BANK)
-            for k in late[:count]:
-                if k < c:
-                    passes(k, (LATE_BANK,))
-                    late.remove(k)
+        def multiply_half(c, ih):
+            quantise_x(c, ih * N_TILE, (ih + 1) * N_TILE)
+            passes(c, ih)
 
-        def load(c):
-            if c + 1 < CHUNKS and c <= pair[0]:
-                load_g(c + 1)
-            if c < pair[0]:
-                load_x(c)
-            elif c == pair[0]:
-                for ih in range(I_TILES):
-                    for k in pair:
-                        load_half_x(k, ih)
-
-        def regroup_g(c):
-            open_g(c)
-            vector_g(c, 0, G_VECTOR)
-            scalar_g(c, G_VECTOR, OUT_F)
-
-        load_g(0)
-        for c in range(RAW_BUFS - 1):
-            load(c)
-        regroup_g(0)
-        for c in range(pair[0]):
-            if c > 0:
-                load(c + RAW_BUFS - 2)
-            if c == SCALES_LOADED:
-                load_scales()
-            if c == SCALES_WIDENED:
-                widen_scales()
-            open_x(c)
-            if c in RELAYED:
-                relay_fill(c)
-            regroup_g(c + 1)
-            if c == 0:
-                quantise_g(0, 0, OUT_F)
-            else:
-                quantise_x(c - 1, 0, IN_F)
-                passes(c - 1, EARLY_BANKS)
-                if c >= RELAYED.stop:
-                    catch_up(c, LATE_PASSES)
-            if c in RELAYED:
-                vector_x(c, RELAY_COLS, RELAY_COLS + RELAY_X_VECTOR)
-                scalar_x(c, RELAY_COLS + RELAY_X_VECTOR, IN_F)
-                relay_copy(c)
-            else:
-                vector_x(c, 0, X_VECTOR)
-                scalar_x(c, X_VECTOR, IN_F)
-            quantise_g(c + 1, 0, OUT_F)
-
-        def scale_out(ot, ih, engine):
+        def scale_out(ot, ih):
             first = ot * GROUPS_PER_ROW + ih * GROUPS_PER_BANK
             scaled = res.tile([P, N_TILE], F32, name="scaled", tag="scaled")
-            if engine == "v":
+            if ot % 2 == 1:
                 nc.vector.tensor_tensor(
                     out=scaled[:].rearrange("p (g w) -> p g w", g=GROUPS_PER_BANK),
                     in0=acc[(ot, ih)][:].rearrange("p (g w) -> p g w", g=GROUPS_PER_BANK),
@@ -291,28 +193,42 @@ def tile_stebitlinear_t_kernel(tc, x, sign_weights, scales, grad_out, out):
                 in_=scaled[:],
             )
 
+        load_g(0)
+        for c in range(RAW_BUFS - 1):
+            load(c)
+        regroup_g(0)
+        for c in range(pair[0]):
+            if c > 0:
+                load(c + RAW_BUFS - 2)
+            if c == SCALES_LOADED:
+                load_scales()
+            if c == SCALES_WIDENED:
+                widen_scales()
+            regroup_g(c + 1)
+            if c == 0:
+                quantise_g(0)
+            else:
+                multiply(c - 1)
+            regroup_x(c)
+            quantise_g(c + 1)
+
         for c in pair:
             open_x(c)
         regroup_g(last)
-        quantise_x(last - 2, 0, IN_F)
-        passes(last - 2, EARLY_BANKS)
-        catch_up(last - 1, CHUNKS)
-        regroup_half_x(last - 1, 0)
-        quantise_g(last, 0, OUT_F)
-        regroup_half_x(last, 0)
-        quantise_x(last - 1, 0, N_TILE)
-        passes(last - 1, LEFT_BANKS)
-        regroup_half_x(last - 1, 1)
-        quantise_x(last, 0, N_TILE)
-        passes(last, LEFT_BANKS)
-        regroup_half_x(last, 1)
-        quantise_x(last - 1, N_TILE, IN_F)
-        passes(last - 1, RIGHT_BANKS)
-        scale_out(0, 0, "s")
-        scale_out(1, 0, "v")
-        quantise_x(last, N_TILE, IN_F)
-        passes(last, RIGHT_BANKS)
-        scale_out(2, 0, "s")
-        scale_out(3, 0, "v")
+        multiply_half(last - 2, left)
+        regroup_half_x(last - 1, left)
+        quantise_g(last)
+        multiply_half(last - 2, right)
+        regroup_half_x(last - 1, right)
+        multiply_half(last - 1, left)
+        regroup_half_x(last, left)
+        multiply_half(last, left)
+        regroup_half_x(last, right)
+        scale_out(0, left)
+        multiply_half(last - 1, right)
+        scale_out(1, left)
+        multiply_half(last, right)
+        scale_out(2, left)
+        scale_out(3, left)
         for ot in range(O_TILES):
-            scale_out(ot, 1, "sv"[ot % 2])
+            scale_out(ot, right)

@@ -23,12 +23,12 @@ O_TILES = OUT_F // M_TILE
 I_TILES = IN_F // N_TILE
 GROUPS_PER_ROW = IN_F // GROUP
 GROUPS_PER_BANK = N_TILE // GROUP
-RUN = 4
+RUN = 8
 
 RAW_BUFS = 6
-G_VECTOR = 248
+G_VECTOR = 256
 X_VECTOR = 512
-HALF_X_VECTOR = 248
+HALF_X_VECTOR = 256
 SCALES_LOADED = 8
 SCALES_WIDENED = 11
 

from contextlib import ExitStack

import concourse.mybir as mybir

BF16 = mybir.dt.bfloat16
F32 = mybir.dt.float32
U32 = mybir.dt.uint32
U8 = mybir.dt.uint8
E4M3X4 = mybir.dt.float8_e4m3fn_x4
E5M2X4 = mybir.dt.float8_e5m2_x4

P = 128
PACK = 4
K_PASS = P * PACK
TOKENS = 8192
IN_F = 1024
OUT_F = 512
GROUP = 128
N_TILE = 512
M_TILE = 128
CHUNKS = TOKENS // K_PASS
O_TILES = OUT_F // M_TILE
I_TILES = IN_F // N_TILE
GROUPS_PER_ROW = IN_F // GROUP
GROUPS_PER_BANK = N_TILE // GROUP
RUN = 8

RAW_BUFS = 6
G_VECTOR = 256
X_VECTOR = 512
HALF_X_VECTOR = 256
SCALES_LOADED = 8
SCALES_WIDENED = 11

FLOPS = 2 * TOKENS * IN_F * OUT_F
BYTES = 2 * TOKENS * (IN_F + OUT_F) + 2 * OUT_F * GROUPS_PER_ROW + 4 * OUT_F * IN_F


def tile_stebitlinear_t_kernel(tc, x, sign_weights, scales, grad_out, out):
    nc = tc.nc
    xt = x.flatten_outer_dims()
    gt = grad_out.flatten_outer_dims()
    last = CHUNKS - 1
    pair = (last - 1, last)
    left, right = range(I_TILES)

    with ExitStack() as ctx:
        const = ctx.enter_context(tc.tile_pool(name="const", bufs=1))
        raw = ctx.enter_context(tc.tile_pool(name="raw", bufs=RAW_BUFS))
        grp = ctx.enter_context(tc.tile_pool(name="grp", bufs=3))
        cod = ctx.enter_context(tc.tile_pool(name="cod", bufs=4))
        res = ctx.enter_context(tc.tile_pool(name="res", bufs=O_TILES * I_TILES))
        psum = ctx.enter_context(tc.psum_pool(name="psum", bufs=1))
        ctx.enter_context(tc.manual_schedule())

        raw_x = {}
        raw_g = {}
        grp_x = {}
        grp_g = {}
        cod_x = {}
        cod_g = {}

        sc_bf = const.tile([P, O_TILES * GROUPS_PER_ROW], BF16, name="sc_bf")
        sc32 = const.tile([P, O_TILES * GROUPS_PER_ROW], F32, name="sc32")

        def load_scales():
            nc.scalar.dma_start(
                out=sc_bf[:].rearrange("p (t g) -> p t g", g=GROUPS_PER_ROW),
                in_=scales.rearrange("(t p g) -> p t g", p=P, g=GROUPS_PER_ROW),
            )

        def widen_scales():
            nc.scalar.activation(out=sc32[:], in_=sc_bf[:], func=mybir.ActivationFunctionType.Copy)

        acc = {}
        for ih in range(I_TILES):
            for ot in range(O_TILES):
                acc[(ot, ih)] = psum.tile([P, N_TILE], F32, name="acc_%d_%d" % (ot, ih))

        def load_g(c):
            rows = slice(c * K_PASS, (c + 1) * K_PASS)
            raw_g[c] = raw.tile([P, PACK, OUT_F], BF16, name="g_raw", tag="g_raw")
            nc.sync.dma_start(out=raw_g[c][:], in_=gt[rows, :].rearrange("(p j) w -> p j w", j=PACK))

        def load_x(c):
            rows = slice(c * K_PASS, (c + 1) * K_PASS)
            raw_x[c] = raw.tile([P, PACK, IN_F], BF16, name="x_raw", tag="x_raw")
            nc.sync.dma_start(out=raw_x[c][:], in_=xt[rows, :].rearrange("(p j) w -> p j w", j=PACK))

        def load(c):
            if c + 1 < CHUNKS:
                load_g(c + 1)
            if c < CHUNKS:
                load_x(c)

        def regroup(dst, src, at, v_cols, width):
            for copy, lo, hi in (
                (nc.vector.tensor_copy, 0, v_cols),
                (nc.scalar.copy, v_cols, width),
            ):
                copy(
                    out=dst[:, at + lo : at + hi, :].rearrange("p (c i) t -> p c t i", i=RUN),
                    in_=src[:, :, lo:hi].rearrange("p t (c i) -> p c t i", i=RUN),
                )

        def regroup_g(c):
            grp_g[c] = grp.tile([P, OUT_F, PACK], BF16, name="g_grp", tag="g_grp", align_bytes=64)
            cod_g[c] = (
                cod.tile([P, OUT_F], U32, name="g_cod", tag="g_cod", align_bytes=64),
                cod.tile([P, OUT_F], U8, name="g_scl", tag="g_scl", align_bytes=64),
            )
            regroup(grp_g[c], raw_g[c], 0, G_VECTOR, OUT_F)

        def open_x(c):
            grp_x[c] = grp.tile([P, IN_F, PACK], BF16, name="x_grp", tag="x_grp", align_bytes=64)
            cod_x[c] = (
                cod.tile([P, IN_F], U32, name="x_cod", tag="x_cod", align_bytes=64),
                cod.tile([P, IN_F], U8, name="x_scl", tag="x_scl", align_bytes=64),
            )

        def regroup_x(c):
            open_x(c)
            regroup(grp_x[c], raw_x[c], 0, X_VECTOR, IN_F)

        def regroup_half_x(c, ih):
            at = ih * N_TILE
            regroup(grp_x[c], raw_x[c][:, :, at : at + N_TILE], at, HALF_X_VECTOR, N_TILE)

        def quantise_g(c):
            g_cod, g_scl = cod_g[c]
            nc.vector.quantize_mx(
                out=g_cod[:].bitcast(E5M2X4),
                scales=g_scl[:],
                in_=grp_g[c][:].rearrange("p w j -> p (w j)"),
            )

        def quantise_x(c, lo, hi):
            x_cod, x_scl = cod_x[c]
            nc.vector.quantize_mx(
                out=x_cod[:, lo:hi].bitcast(E4M3X4),
                scales=x_scl[:, lo:hi],
                in_=grp_x[c][:, lo:hi, :].rearrange("p w j -> p (w j)"),
            )

        def passes(c, ih):
            g_cod, g_scl = cod_g[c]
            x_cod, x_scl = cod_x[c]
            n_cols = slice(ih * N_TILE, (ih + 1) * N_TILE)
            for ot in range(O_TILES):
                m_cols = slice(ot * M_TILE, (ot + 1) * M_TILE)
                nc.tensor.matmul_mx(
                    out=acc[(ot, ih)][:],
                    lhsT=g_cod[:, m_cols].bitcast(E5M2X4),
                    lhsT_scale=g_scl[:, m_cols],
                    rhs=x_cod[:, n_cols].bitcast(E4M3X4),
                    rhs_scale=x_scl[:, n_cols],
                    start=(c == 0),
                    stop=(c == last),
                )

        def multiply(c):
            quantise_x(c, 0, IN_F)
            for ih in range(I_TILES):
                passes(c, ih)

        def multiply_half(c, ih):
            quantise_x(c, ih * N_TILE, (ih + 1) * N_TILE)
            passes(c, ih)

        def scale_out(ot, ih):
            first = ot * GROUPS_PER_ROW + ih * GROUPS_PER_BANK
            scaled = res.tile([P, N_TILE], F32, name="scaled", tag="scaled")
            if ot % 2 == 1:
                nc.vector.tensor_tensor(
                    out=scaled[:].rearrange("p (g w) -> p g w", g=GROUPS_PER_BANK),
                    in0=acc[(ot, ih)][:].rearrange("p (g w) -> p g w", g=GROUPS_PER_BANK),
                    in1=sc32[:, first : first + GROUPS_PER_BANK]
                    .unsqueeze(2)
                    .to_broadcast([P, GROUPS_PER_BANK, GROUP]),
                    op=mybir.AluOpType.mult,
                )
            else:
                for g in range(GROUPS_PER_BANK):
                    cols = slice(g * GROUP, (g + 1) * GROUP)
                    nc.scalar.activation(
                        out=scaled[:, cols],
                        in_=acc[(ot, ih)][:, cols],
                        func=mybir.ActivationFunctionType.Copy,
                        scale=sc32[:, first + g : first + g + 1],
                    )
            nc.sync.dma_start(
                out=out[ot * M_TILE : (ot + 1) * M_TILE, ih * N_TILE : (ih + 1) * N_TILE],
                in_=scaled[:],
            )

        load_g(0)
        for c in range(RAW_BUFS - 1):
            load(c)
        regroup_g(0)
        for c in range(pair[0]):
            if c > 0:
                load(c + RAW_BUFS - 2)
            if c == SCALES_LOADED:
                load_scales()
            if c == SCALES_WIDENED:
                widen_scales()
            regroup_g(c + 1)
            if c == 0:
                quantise_g(0)
            else:
                multiply(c - 1)
            regroup_x(c)
            quantise_g(c + 1)

        for c in pair:
            open_x(c)
        regroup_g(last)
        multiply_half(last - 2, left)
        regroup_half_x(last - 1, left)
        quantise_g(last)
        multiply_half(last - 2, right)
        regroup_half_x(last - 1, right)
        multiply_half(last - 1, left)
        regroup_half_x(last, left)
        multiply_half(last, left)
        regroup_half_x(last, right)
        scale_out(0, left)
        multiply_half(last - 1, right)
        scale_out(1, left)
        multiply_half(last, right)
        scale_out(2, left)
        scale_out(3, left)
        for ot in range(O_TILES):
            scale_out(ot, right)
